import numpy as np
import ml_dtypes

BF16 = ml_dtypes.bfloat16


def bf(x):
    return np.asarray(x, np.float32).astype(BF16)


def f32(x):
    return np.asarray(x, np.float32)


def f64(x):
    return np.asarray(x).astype(np.float64)


def striped(idx):
    return np.tile(idx.reshape(-1, 16).T, (8, 1))


C, S, N = 128, 4096, 2048
POOL_B = 0.25


def sigmoid(v):
    return 1.0 / (1.0 + np.exp(-v))


def setup_inputs():
    return {"x": f32(np.random.standard_normal((C, S))), "pool_w": f32(np.random.standard_normal((C, 1)) / np.sqrt(C)), "offs": striped(np.random.permutation(np.tile(np.arange(S), 2))[:N])}


def reference(x, pool_w, offs):
    idx = offs[:16].T.reshape(-1)
    h = f64(x)[:, idx]
    t = (h * f64(pool_w)).sum(axis=0, keepdims=True) + POOL_B
    return h * sigmoid(t)

@@ -1,0 +1,61 @@
+import concourse.mybir as mybir
+
+F32 = mybir.dt.float32
+BF16 = mybir.dt.bfloat16
+U16 = mybir.dt.uint16
+MULT = mybir.AluOpType.mult
+SIGMOID = mybir.ActivationFunctionType.Sigmoid
+
+C = 128
+S = 4096
+N = 2048
+POOL_B = 0.25
+PIECE = 512
+N_PIECES = N // PIECE
+
+FLOPS = 3 * C * N
+
+
+def tile_mymodel_kernel(tc, x, pool_w, offs, out):
+    nc = tc.nc
+    with (
+        tc.tile_pool(name="held", bufs=1) as held,
+        tc.tile_pool(name="work", bufs=N_PIECES) as work,
+        tc.psum_pool(name="psum", bufs=N_PIECES) as psum,
+    ):
+        offsets = held.tile([C, N // 16], U16, name="offsets")
+        nc.sync.dma_start(offsets[:], offs)
+
+        table = held.tile([C, S], F32, name="table")
+        nc.sync.dma_start(table[:, : S // 2], x[:, : S // 2])
+        nc.scalar.dma_start(table[:, S // 2 :], x[:, S // 2 :])
+
+        w_column = held.tile([C, 1], F32, name="w_column")
+        nc.gpsimd.dma_start(w_column[:], pool_w)
+        w_wide = held.tile([C, PIECE], F32, name="w_wide")
+        nc.gpsimd.tensor_copy(w_wide[:], w_column[:].to_broadcast([C, PIECE]))
+
+        ones = held.tile([C, C], BF16, name="ones")
+        nc.gpsimd.memset(ones[:], 1.0)
+        bias = held.tile([C, 1], F32, name="bias")
+        nc.gpsimd.memset(bias[:], POOL_B)
+
+        def piece_of_list(p):
+            return offsets[:, p * (PIECE // 16) : (p + 1) * (PIECE // 16)]
+
+        weights = []
+        for p in range(N_PIECES):
+            product = work.tile([C, PIECE], F32, name="product")
+            nc.vector.tensor_tensor(product[:], table[:].indirect(piece_of_list(p)), w_wide[:], MULT)
+            rounded = work.tile([C, PIECE], BF16, name="rounded")
+            nc.scalar.copy(rounded[:], product[:])
+            sums = psum.tile([C, PIECE], F32, name="sums")
+            nc.tensor.matmul(sums[:], ones[:], rounded[:], start=True, stop=True)
+            weight = work.tile([C, PIECE], F32, name="weight")
+            nc.scalar.activation(weight[:], sums[:], SIGMOID, bias=bias[:])
+            weights.append(weight)
+
+        for p in range(N_PIECES):
+            result = work.tile([C, PIECE], F32, name="result")
+            nc.vector.tensor_tensor(result[:], table[:].indirect(piece_of_list(p)), weights[p][:], MULT)
+            nc.sync.dma_start(out[:, p * PIECE : (p + 1) * PIECE], result[:])

@@ -26,12 +26,13 @@ def tile_mymodel_kernel(tc, x, pool_w, offs, out):
         offsets = held.tile([C, N // 16], U16, name="offsets")
         nc.sync.dma_start(offsets[:], offs)
 
+        w_column = held.tile([C, 1], F32, name="w_column")
+        nc.scalar.dma_start(w_column[:], pool_w)
+
         table = held.tile([C, S], F32, name="table")
         nc.sync.dma_start(table[:, : S // 2], x[:, : S // 2])
         nc.scalar.dma_start(table[:, S // 2 :], x[:, S // 2 :])
 
-        w_column = held.tile([C, 1], F32, name="w_column")
-        nc.gpsimd.dma_start(w_column[:], pool_w)
         w_wide = held.tile([C, PIECE], F32, name="w_wide")
         nc.gpsimd.tensor_copy(w_wide[:], w_column[:].to_broadcast([C, PIECE]))
 

@@ -40,6 +40,8 @@ def tile_mymodel_kernel(tc, x, pool_w, offs, out):
         nc.gpsimd.memset(ones[:], 1.0)
         bias = held.tile([C, 1], F32, name="bias")
         nc.gpsimd.memset(bias[:], POOL_B)
+        warm = held.tile([C, 1], F32, name="warm")
+        nc.scalar.activation(warm[:], bias[:], SIGMOID)
 
         def piece_of_list(p):
             return offsets[:, p * (PIECE // 16) : (p + 1) * (PIECE // 16)]

@@ -46,17 +46,26 @@ def tile_mymodel_kernel(tc, x, pool_w, offs, out):
         def piece_of_list(p):
             return offsets[:, p * (PIECE // 16) : (p + 1) * (PIECE // 16)]
 
-        weights = []
-        for p in range(N_PIECES):
+        def rounded_product(p):
             product = work.tile([C, PIECE], F32, name="product")
             nc.vector.tensor_tensor(product[:], table[:].indirect(piece_of_list(p)), w_wide[:], MULT)
             rounded = work.tile([C, PIECE], BF16, name="rounded")
             nc.scalar.copy(rounded[:], product[:])
+            return rounded
+
+        def sigmoid_weight(rounded):
             sums = psum.tile([C, PIECE], F32, name="sums")
             nc.tensor.matmul(sums[:], ones[:], rounded[:], start=True, stop=True)
             weight = work.tile([C, PIECE], F32, name="weight")
             nc.scalar.activation(weight[:], sums[:], SIGMOID, bias=bias[:])
-            weights.append(weight)
+            return weight
+
+        weights = []
+        rounded_ahead = rounded_product(0)
+        for p in range(1, N_PIECES):
+            rounded_now, rounded_ahead = rounded_ahead, rounded_product(p)
+            weights.append(sigmoid_weight(rounded_now))
+        weights.append(sigmoid_weight(rounded_ahead))
 
         for p in range(N_PIECES):
             result = work.tile([C, PIECE], F32, name="result")

@@ -21,6 +21,7 @@ def tile_mymodel_kernel(tc, x, pool_w, offs, out):
     with (
         tc.tile_pool(name="held", bufs=1) as held,
         tc.tile_pool(name="work", bufs=N_PIECES) as work,
+        tc.tile_pool(name="pair", bufs=2) as pair,
         tc.psum_pool(name="psum", bufs=N_PIECES) as psum,
     ):
         offsets = held.tile([C, N // 16], U16, name="offsets")
@@ -46,26 +47,17 @@ def tile_mymodel_kernel(tc, x, pool_w, offs, out):
         def piece_of_list(p):
             return offsets[:, p * (PIECE // 16) : (p + 1) * (PIECE // 16)]
 
-        def rounded_product(p):
+        weights = []
+        for p in range(N_PIECES):
             product = work.tile([C, PIECE], F32, name="product")
             nc.vector.tensor_tensor(product[:], table[:].indirect(piece_of_list(p)), w_wide[:], MULT)
-            rounded = work.tile([C, PIECE], BF16, name="rounded")
+            rounded = pair.tile([C, PIECE], BF16, name="rounded")
             nc.scalar.copy(rounded[:], product[:])
-            return rounded
-
-        def sigmoid_weight(rounded):
             sums = psum.tile([C, PIECE], F32, name="sums")
             nc.tensor.matmul(sums[:], ones[:], rounded[:], start=True, stop=True)
             weight = work.tile([C, PIECE], F32, name="weight")
             nc.scalar.activation(weight[:], sums[:], SIGMOID, bias=bias[:])
-            return weight
-
-        weights = []
-        rounded_ahead = rounded_product(0)
-        for p in range(1, N_PIECES):
-            rounded_now, rounded_ahead = rounded_ahead, rounded_product(p)
-            weights.append(sigmoid_weight(rounded_now))
-        weights.append(sigmoid_weight(rounded_ahead))
+            weights.append(weight)
 
         for p in range(N_PIECES):
             result = work.tile([C, PIECE], F32, name="result")

@@ -12,6 +12,7 @@ N = 2048
 POOL_B = 0.25
 PIECE = 512
 N_PIECES = N // PIECE
+LAST = 128
 
 FLOPS = 3 * C * N
 
@@ -59,7 +60,15 @@ def tile_mymodel_kernel(tc, x, pool_w, offs, out):
             nc.scalar.activation(weight[:], sums[:], SIGMOID, bias=bias[:])
             weights.append(weight)
 
-        for p in range(N_PIECES):
-            result = work.tile([C, PIECE], F32, name="result")
-            nc.vector.tensor_tensor(result[:], table[:].indirect(piece_of_list(p)), weights[p][:], MULT)
-            nc.sync.dma_start(out[:, p * PIECE : (p + 1) * PIECE], result[:])
+        result = held.tile([C, N], F32, name="result")
+        cuts = [(p, 0, PIECE) for p in range(N_PIECES - 1)]
+        cuts += [(N_PIECES - 1, 0, PIECE - LAST), (N_PIECES - 1, PIECE - LAST, LAST)]
+        for p, start, width in cuts:
+            first = p * PIECE + start
+            nc.vector.tensor_tensor(
+                result[:, first : first + width],
+                table[:].indirect(offsets[:, first // 16 : (first + width) // 16]),
+                weights[p][:, start : start + width],
+                MULT,
+            )
+            nc.sync.dma_start(out[:, first : first + width], result[:, first : first + width])

@@ -12,7 +12,7 @@ N = 2048
 POOL_B = 0.25
 PIECE = 512
 N_PIECES = N // PIECE
-LAST = 128
+LAST = 256
 
 FLOPS = 3 * C * N
 

@@ -71,4 +71,7 @@ def tile_mymodel_kernel(tc, x, pool_w, offs, out):
                 weights[p][:, start : start + width],
                 MULT,
             )
-            nc.sync.dma_start(out[:, first : first + width], result[:, first : first + width])
+            if first == 0:
+                continue
+            stored_from = 0 if first == PIECE else first
+            nc.sync.dma_start(out[:, stored_from : first + width], result[:, stored_from : first + width])

@@ -10,8 +10,7 @@ C = 128
 S = 4096
 N = 2048
 POOL_B = 0.25
-PIECE = 512
-N_PIECES = N // PIECE
+BLOCK = 256
 LAST = 256
 
 FLOPS = 3 * C * N
@@ -21,9 +20,8 @@ def tile_mymodel_kernel(tc, x, pool_w, offs, out):
     nc = tc.nc
     with (
         tc.tile_pool(name="held", bufs=1) as held,
-        tc.tile_pool(name="work", bufs=N_PIECES) as work,
-        tc.tile_pool(name="pair", bufs=2) as pair,
-        tc.psum_pool(name="psum", bufs=N_PIECES) as psum,
+        tc.tile_pool(name="pair", bufs=4) as pair,
+        tc.psum_pool(name="psum", bufs=N // BLOCK) as psum,
     ):
         offsets = held.tile([C, N // 16], U16, name="offsets")
         nc.sync.dma_start(offsets[:], offs)
@@ -35,8 +33,8 @@ def tile_mymodel_kernel(tc, x, pool_w, offs, out):
         nc.sync.dma_start(table[:, : S // 2], x[:, : S // 2])
         nc.scalar.dma_start(table[:, S // 2 :], x[:, S // 2 :])
 
-        w_wide = held.tile([C, PIECE], F32, name="w_wide")
-        nc.gpsimd.tensor_copy(w_wide[:], w_column[:].to_broadcast([C, PIECE]))
+        w_wide = held.tile([C, N // 2], F32, name="w_wide")
+        nc.vector.tensor_copy(w_wide[:], w_column[:].to_broadcast([C, N // 2]))
 
         ones = held.tile([C, C], BF16, name="ones")
         nc.gpsimd.memset(ones[:], 1.0)
@@ -45,33 +43,23 @@ def tile_mymodel_kernel(tc, x, pool_w, offs, out):
         warm = held.tile([C, 1], F32, name="warm")
         nc.scalar.activation(warm[:], bias[:], SIGMOID)
 
-        def piece_of_list(p):
-            return offsets[:, p * (PIECE // 16) : (p + 1) * (PIECE // 16)]
+        def looked_up(first, width):
+            return table[:].indirect(offsets[:, first // 16 : (first + width) // 16])
 
-        weights = []
-        for p in range(N_PIECES):
-            product = work.tile([C, PIECE], F32, name="product")
-            nc.vector.tensor_tensor(product[:], table[:].indirect(piece_of_list(p)), w_wide[:], MULT)
-            rounded = pair.tile([C, PIECE], BF16, name="rounded")
-            nc.scalar.copy(rounded[:], product[:])
-            sums = psum.tile([C, PIECE], F32, name="sums")
-            nc.tensor.matmul(sums[:], ones[:], rounded[:], start=True, stop=True)
-            weight = work.tile([C, PIECE], F32, name="weight")
-            nc.scalar.activation(weight[:], sums[:], SIGMOID, bias=bias[:])
-            weights.append(weight)
+        product = held.tile([C, N], F32, name="product")
+        weight = held.tile([C, N], F32, name="weight")
+        first_cuts = [0, N // 4, N // 2, N]
+        for first, end in zip(first_cuts[:-1], first_cuts[1:]):
+            nc.vector.tensor_tensor(product[:, first:end], looked_up(first, end - first), w_wide[:, : end - first], MULT)
+            for b in range(first, end, BLOCK):
+                rounded = pair.tile([C, BLOCK], BF16, name="rounded")
+                nc.scalar.copy(rounded[:], product[:, b : b + BLOCK])
+                sums = psum.tile([C, BLOCK], F32, name="sums")
+                nc.tensor.matmul(sums[:], ones[:], rounded[:], start=True, stop=True)
+                nc.scalar.activation(weight[:, b : b + BLOCK], sums[:], SIGMOID, bias=bias[:])
 
         result = held.tile([C, N], F32, name="result")
-        cuts = [(p, 0, PIECE) for p in range(N_PIECES - 1)]
-        cuts += [(N_PIECES - 1, 0, PIECE - LAST), (N_PIECES - 1, PIECE - LAST, LAST)]
-        for p, start, width in cuts:
-            first = p * PIECE + start
-            nc.vector.tensor_tensor(
-                result[:, first : first + width],
-                table[:].indirect(offsets[:, first // 16 : (first + width) // 16]),
-                weights[p][:, start : start + width],
-                MULT,
-            )
-            if first == 0:
-                continue
-            stored_from = 0 if first == PIECE else first
-            nc.sync.dma_start(out[:, stored_from : first + width], result[:, stored_from : first + width])
+        cuts = [0, N // 2, 3 * N // 4, N - LAST, N]
+        for first, end in zip(cuts[:-1], cuts[1:]):
+            nc.vector.tensor_tensor(result[:, first:end], looked_up(first, end - first), weight[:, first:end], MULT)
+            nc.sync.dma_start(out[:, first:end], result[:, first:end])

import concourse.mybir as mybir

F32 = mybir.dt.float32
BF16 = mybir.dt.bfloat16
U16 = mybir.dt.uint16
MULT = mybir.AluOpType.mult
SIGMOID = mybir.ActivationFunctionType.Sigmoid

C = 128
S = 4096
N = 2048
POOL_B = 0.25
BLOCK = 256
LAST = 256

FLOPS = 3 * C * N


def tile_mymodel_kernel(tc, x, pool_w, offs, out):
    nc = tc.nc
    with (
        tc.tile_pool(name="held", bufs=1) as held,
        tc.tile_pool(name="pair", bufs=4) as pair,
        tc.psum_pool(name="psum", bufs=N // BLOCK) as psum,
    ):
        offsets = held.tile([C, N // 16], U16, name="offsets")
        nc.sync.dma_start(offsets[:], offs)

        w_column = held.tile([C, 1], F32, name="w_column")
        nc.scalar.dma_start(w_column[:], pool_w)

        table = held.tile([C, S], F32, name="table")
        nc.sync.dma_start(table[:, : S // 2], x[:, : S // 2])
        nc.scalar.dma_start(table[:, S // 2 :], x[:, S // 2 :])

        w_wide = held.tile([C, N // 2], F32, name="w_wide")
        nc.vector.tensor_copy(w_wide[:], w_column[:].to_broadcast([C, N // 2]))

        ones = held.tile([C, C], BF16, name="ones")
        nc.gpsimd.memset(ones[:], 1.0)
        bias = held.tile([C, 1], F32, name="bias")
        nc.gpsimd.memset(bias[:], POOL_B)
        warm = held.tile([C, 1], F32, name="warm")
        nc.scalar.activation(warm[:], bias[:], SIGMOID)

        def looked_up(first, width):
            return table[:].indirect(offsets[:, first // 16 : (first + width) // 16])

        product = held.tile([C, N], F32, name="product")
        weight = held.tile([C, N], F32, name="weight")
        first_cuts = [0, N // 4, N // 2, N]
        for first, end in zip(first_cuts[:-1], first_cuts[1:]):
            nc.vector.tensor_tensor(product[:, first:end], looked_up(first, end - first), w_wide[:, : end - first], MULT)
            for b in range(first, end, BLOCK):
                rounded = pair.tile([C, BLOCK], BF16, name="rounded")
                nc.scalar.copy(rounded[:], product[:, b : b + BLOCK])
                sums = psum.tile([C, BLOCK], F32, name="sums")
                nc.tensor.matmul(sums[:], ones[:], rounded[:], start=True, stop=True)
                nc.scalar.activation(weight[:, b : b + BLOCK], sums[:], SIGMOID, bias=bias[:])

        result = held.tile([C, N], F32, name="result")
        cuts = [0, N // 2, 3 * N // 4, N - LAST, N]
        for first, end in zip(cuts[:-1], cuts[1:]):
            nc.vector.tensor_tensor(result[:, first:end], looked_up(first, end - first), weight[:, first:end], MULT)
            nc.sync.dma_start(out[:, first:end], result[:, first:end])
